import numpy as np
import ml_dtypes


def mxq(x, axis, fmt="e4m3"):
    dtype, down = {"e4m3": (ml_dtypes.float8_e4m3fn, 7), "e5m2": (ml_dtypes.float8_e5m2, 14)}[fmt]
    v = np.moveaxis(np.asarray(x, np.float32).astype(ml_dtypes.bfloat16).astype(np.float64), axis, -1)
    blocks = v.reshape(v.shape[:-1] + (-1, 32))
    amax = np.abs(blocks).max(-1, keepdims=True)
    byte = np.maximum(np.where(amax > 0, np.frexp(amax)[1] - 1 + 127, 0) - down, 1)
    scale = np.exp2(byte - 127.0)
    codes = (blocks / scale).astype(np.float32).astype(dtype).astype(np.float64)
    return np.moveaxis((codes * scale).reshape(v.shape), -1, axis)


WIDE = False


def mx_kscale(k):
    if not WIDE:
        return np.ones(k)
    levels = np.array([10, -10, 5, -5, 0])
    if k % 512:
        return np.exp2(np.random.permutation(np.resize(levels, k // 32))).repeat(32)
    a = np.empty((k // 512, 16))
    for p in range(k // 512):
        a[p, :8] = np.random.permutation(np.resize(levels, 8))
        for g in range(8):
            far = levels[np.abs(levels - a[p, g]) >= 10]
            a[p, g + 8] = far[np.random.randint(len(far))]
    return np.exp2(a.ravel()).repeat(32)


BF16 = ml_dtypes.bfloat16


def bf(x):
    return np.asarray(x, np.float32).astype(BF16)


def f64(x):
    return np.asarray(x).astype(np.float64)


N, M, D, K = 1024, 1024, 512, 3
SLOPE = 0.01


def leaky_relu(v):
    return np.where(v >= 0.0, v, SLOPE * v)


def draw0():
    s, t = mx_kscale(D), mx_kscale(D)
    return {"p_last": bf(leaky_relu(np.random.standard_normal((M, D)) * 0.3 - 0.1) * s),
            "q_last": bf(leaky_relu(np.random.standard_normal((N, D)) * 0.3 - 0.1) / t),
            "distance_matrix": bf(np.random.uniform(size=(M, N)) + 0.1),
            "Wd": bf(np.random.standard_normal((D, D)) / np.sqrt(D) * t[:, None] / s[None, :]),
            "bd": bf(np.random.standard_normal(D) * 0.1 * t),
            "a": bf(np.random.uniform(0.5, 1.0, size=(1,))),
            "b": bf(-np.random.uniform(0.5, 1.0, size=(1,))),
            "c": bf(-np.random.uniform(0.5, 1.0, size=(1,)))}


def core(p_last, q_last, distance_matrix, Wd, bd, a, b, c):
    dist = f64(distance_matrix)
    fx = f64(a)[0] * dist ** f64(b)[0] * np.exp(f64(c)[0] * dist)
    dec = (mxq(f64(p_last), 1, "e4m3") @ mxq(f64(Wd).T, 0, "e4m3")) + f64(bd)
    return (mxq(dec, 1, "e4m3") @ mxq(f64(q_last).T, 0, "e4m3")) * fx


def e4m3fn_bytes(y):
    return np.clip(np.asarray(y, np.float64), -448.0, 448.0).astype(np.float32).astype(ml_dtypes.float8_e4m3fn).view(np.uint8)


def e4m3fn_values(b):
    return np.asarray(b, np.uint8).view(ml_dtypes.float8_e4m3fn).astype(np.float64)


def setup_inputs():
    d = draw0()
    x0 = np.asarray(d['q_last']).astype(np.float64)
    s = (np.max(np.abs(x0), axis=(0,), keepdims=True) / 448.0).astype(np.float32)
    out = {}
    for k, v in d.items():
        if k == 'q_last':
            out['q_last_bytes'] = e4m3fn_bytes(x0 / s.astype(np.float64))
            out['q_last_scale'] = s
        else:
            out[k] = v
    return out


def reference(p_last, q_last_bytes, q_last_scale, distance_matrix, Wd, bd, a, b, c):
    return core(p_last, e4m3fn_values(q_last_bytes) * q_last_scale.astype(np.float64), distance_matrix, Wd, bd, a, b, c)

@@ -1,0 +1,267 @@
+from contextlib import ExitStack
+
+import concourse.mybir as mybir
+from concourse.masks import make_identity
+
+NODES, K = 1024, 512
+P = 128
+R = NODES // P
+FLOPS = 2 * NODES * K * K + 2 * NODES * NODES * K
+
+F32 = mybir.dt.float32
+BF16 = mybir.dt.bfloat16
+U32 = mybir.dt.uint32
+U8 = mybir.dt.uint8
+FP8 = mybir.dt.float8_e4m3fn
+FP8X4 = mybir.dt.float8_e4m3fn_x4
+ALU = mybir.AluOpType
+ACT = mybir.ActivationFunctionType
+
+
+def tile_gglr_pb_kernel(tc, p_last, q_bytes, q_scale, dist, wd, bd, a, b, c, out):
+    nc = tc.nc
+    with ExitStack() as ctx:
+        keep = ctx.enter_context(tc.tile_pool(name="keep", bufs=1))
+        psum = ctx.enter_context(tc.psum_pool(name="psum", bufs=8))
+        ctx.enter_context(tc.manual_schedule())
+
+        ident = keep.tile([P, P], F32)
+        ident_bf = keep.tile([P, P], BF16)
+        diag = keep.tile([P, P], F32)
+        warm = keep.tile([P, 1], F32)
+        s4 = keep.tile([P, 4], F32)
+        bias = keep.tile([P, 4], BF16)
+        a_bf = keep.tile([P, 1], BF16)
+        b_bf = keep.tile([P, 1], BF16)
+        c_bf = keep.tile([P, 1], BF16)
+        gain = keep.tile([P, 1], F32)
+        c_abs = keep.tile([P, 1], F32)
+        c_low = keep.tile([P, 1], F32)
+        decay = keep.tile([P, 1], F32)
+        c_inv = keep.tile([P, 1], F32)
+        ratio = keep.tile([P, 1], F32)
+        scale_row = keep.tile([P, K], F32, align_bytes=64)
+        q_raw = keep.tile([P, R, K], U8, align_bytes=64)
+        q_val = keep.tile([P, R, K], BF16, align_bytes=64)
+        w_raw = keep.tile([P, 4, K], BF16, align_bytes=64)
+        p_raw = keep.tile([P, R, K], BF16, align_bytes=64)
+        d_raw = keep.tile([P, R, NODES], BF16, align_bytes=64)
+        w_grp = keep.tile([P, K, 4], BF16, align_bytes=64)
+        p_grp = keep.tile([P, NODES, 4], BF16, align_bytes=64)
+        q_grp = keep.tile([P, NODES, 4], BF16, align_bytes=64)
+        dec_grp = keep.tile([P, NODES, 4], BF16, align_bytes=64)
+        w_code = keep.tile([P, K], U32, align_bytes=64)
+        w_exp = keep.tile([P, K], U8, align_bytes=64)
+        p_code = keep.tile([P, NODES], U32, align_bytes=64)
+        p_exp = keep.tile([P, NODES], U8, align_bytes=64)
+        q_code = keep.tile([P, NODES], U32, align_bytes=64)
+        q_exp = keep.tile([P, NODES], U8, align_bytes=64)
+        dec_code = keep.tile([P, NODES], U32, align_bytes=64)
+        dec_exp = keep.tile([P, NODES], U8, align_bytes=64)
+        lnd = keep.tile([P, R, NODES], F32, align_bytes=64)
+        fx = keep.tile([P, R, NODES], F32, align_bytes=64)
+        res = keep.tile([P, R, NODES], F32, align_bytes=64)
+
+        nc.sync.dma_start(out=s4[:], in_=q_scale.rearrange("o (p t) -> p (o t)", t=4))
+        q_src = q_bytes.rearrange("(r p) k -> p r k", p=P)
+        p_src = p_last.rearrange("(p r) k -> p r k", r=R)
+        d_src = dist.rearrange("(p r) n -> p r n", r=R)
+        o_dst = out.rearrange("(p r) n -> p r n", r=R)
+        nc.sync.dma_start(out=q_raw[:, 0:4, :], in_=q_src[:, 0:4, :])
+        nc.sync.dma_start(out=d_raw[:, 0:1, :], in_=d_src[:, 0:1, :])
+        nc.sync.dma_start(out=w_raw[:], in_=wd.rearrange("(m t) k -> m t k", t=4))
+        nc.sync.dma_start(out=q_raw[:, 4:8, :], in_=q_src[:, 4:8, :])
+        nc.sync.dma_start(out=d_raw[:, 1:2, :], in_=d_src[:, 1:2, :])
+        nc.sync.dma_start(out=p_raw[:, 0:4, :], in_=p_src[:, 0:4, :])
+        nc.sync.dma_start(out=p_raw[:, 4:8, :], in_=p_src[:, 4:8, :])
+        for r in range(2, R, 2):
+            nc.sync.dma_start(out=d_raw[:, r : r + 2, :], in_=d_src[:, r : r + 2, :])
+        nc.scalar.dma_start(out=c_bf[:], in_=c.partition_broadcast(P))
+        nc.scalar.dma_start(out=b_bf[:], in_=b.partition_broadcast(P))
+        nc.scalar.dma_start(out=a_bf[:], in_=a.partition_broadcast(P))
+        nc.scalar.dma_start(out=bias[:], in_=bd.rearrange("(p t) -> p t", t=4))
+
+        nc.vector.memset(warm[:], 1.0)
+        nc.scalar.activation(out=warm[:], in_=warm[:], func=ACT.Ln)
+        make_identity(nc, ident[:])
+        make_identity(nc, ident_bf[:])
+
+        def transpose_pair(srcs):
+            bank = psum.tile([P, 512], F32, name="bank", tag="bank")
+            halves = bank[:].rearrange("p (u j) -> p u j", u=2)
+            for i, src in enumerate(srcs):
+                words = src.bitcast(F32)
+                for u in range(2):
+                    nc.tensor.transpose(halves[:, u, i * P : (i + 1) * P], words[:, u::2], ident[:])
+            return bank
+
+        def unload(bank, grp, col):
+            dst = grp[:, col : col + 256, :].rearrange("p j e -> p (j e)").bitcast(F32)
+            nc.scalar.copy(
+                out=dst.rearrange("p (j u) -> p j u", u=2),
+                in_=bank[:].rearrange("p (u j) -> p j u", u=2),
+            )
+
+        def quantize(grp, code, exps, lo, hi):
+            nc.vector.quantize_mx(
+                out=code[:, lo:hi].bitcast(FP8X4),
+                scales=exps[:, lo:hi],
+                in_=grp[:, lo:hi, :].rearrange("p j e -> p (j e)"),
+            )
+
+        def log(r):
+            nc.scalar.activation(out=lnd[:, r, :], in_=d_raw[:, r, :], func=ACT.Ln)
+
+        def exponent(r):
+            nc.vector.scalar_tensor_tensor(
+                out=lnd[:, r, :], in0=lnd[:, r, :], scalar=ratio[:], in1=d_raw[:, r, :], op0=ALU.mult, op1=ALU.add
+            )
+
+        def exponent_pe(r):
+            banks = []
+            for h in range(2):
+                bank = psum.tile([P, 512], F32, name="bank", tag="bank")
+                qs = slice(h * 512, (h + 1) * 512)
+                nc.tensor.matmul(bank[:], lhsT=ident_bf[:], rhs=d_raw[:, r, qs], start=True, stop=False)
+                nc.tensor.matmul(bank[:], lhsT=diag[:], rhs=lnd[:, r, qs], start=False, stop=True)
+                banks.append(bank)
+            return banks
+
+        def exp_pe(r, banks):
+            for h in range(2):
+                qs = slice(h * 512, (h + 1) * 512)
+                nc.scalar.activation(out=fx[:, r, qs], in_=banks[h][:], func=ACT.Exp, scale=decay[:])
+
+        def exp(r):
+            nc.scalar.activation(out=fx[:, r, :], in_=lnd[:, r, :], func=ACT.Exp, scale=decay[:])
+
+        def product(r):
+            nc.vector.tensor_tensor(out=q_val[:, r, :], in0=q_raw[:, r, :].bitcast(FP8), in1=scale_row[:], op=ALU.mult)
+
+        def stage1(r):
+            bank = psum.tile([P, 512], F32, name="bank", tag="bank")
+            cols = slice(r * P, (r + 1) * P)
+            for t in range(4):
+                ws = slice(t * P, (t + 1) * P)
+                nc.tensor.matmul_mx(
+                    out=bank[:, ws],
+                    lhsT=w_code[:, ws].bitcast(FP8X4),
+                    lhsT_scale=w_exp[:, ws],
+                    rhs=p_code[:, cols].bitcast(FP8X4),
+                    rhs_scale=p_exp[:, cols],
+                    start=True,
+                    stop=True,
+                )
+            return bank
+
+        def add_bias(r, bank):
+            nc.vector.tensor_tensor(
+                out=dec_grp[:, r * P : (r + 1) * P, :],
+                in0=bank[:].rearrange("p (t j) -> p j t", t=4),
+                in1=bias[:].unsqueeze(1).to_broadcast([P, P, 4]),
+                op=ALU.add,
+            )
+
+        def stage2(r):
+            cols = slice(r * P, (r + 1) * P)
+            banks = []
+            for h in range(2):
+                bank = psum.tile([P, 512], F32, name="bank", tag="bank")
+                qs = slice(h * 512, (h + 1) * 512)
+                nc.tensor.matmul_mx(
+                    out=bank[:],
+                    lhsT=dec_code[:, cols].bitcast(FP8X4),
+                    lhsT_scale=dec_exp[:, cols],
+                    rhs=q_code[:, qs].bitcast(FP8X4),
+                    rhs_scale=q_exp[:, qs],
+                    start=True,
+                    stop=True,
+                )
+                banks.append(bank)
+            return banks
+
+        def finish(r, h, bank):
+            qs = slice(h * 512, (h + 1) * 512)
+            nc.vector.scalar_tensor_tensor(
+                out=res[:, r, qs], in0=bank[:], scalar=gain[:], in1=fx[:, r, qs], op0=ALU.mult, op1=ALU.mult
+            )
+
+        bank = psum.tile([P, 512], F32, name="bank", tag="bank")
+        for t in range(4):
+            nc.tensor.transpose(bank[:, t * P : (t + 1) * P], s4[:, t : t + 1].to_broadcast([P, P]), ident[:])
+        nc.vector.tensor_copy(
+            out=scale_row[:].rearrange("p (j t) -> p j t", t=4), in_=bank[:].rearrange("p (t j) -> p j t", t=4)
+        )
+
+        for r in range(4):
+            product(r)
+        nc.vector.tensor_scalar(out=c_abs[:], in0=c_bf[:], scalar1=-1.0, scalar2=None, op0=ALU.mult)
+        nc.vector.tensor_copy(out=gain[:], in_=a_bf[:])
+        nc.vector.tensor_tensor(out=c_abs[:], in0=c_abs[:], in1=c_bf[:], op=ALU.max)
+        product(4)
+        nc.vector.tensor_scalar(out=c_low[:], in0=c_abs[:], scalar1=1e-20, scalar2=2e-20, op0=ALU.is_lt, op1=ALU.mult)
+        product(5)
+        nc.vector.tensor_tensor(out=decay[:], in0=c_low[:], in1=c_bf[:], op=ALU.add)
+        product(6)
+        nc.vector.reciprocal(out=c_inv[:], in_=decay[:])
+        product(7)
+        nc.vector.tensor_tensor(out=ratio[:], in0=c_inv[:], in1=b_bf[:], op=ALU.mult)
+        nc.gpsimd.tensor_scalar(out=diag[:], in0=ident[:], scalar1=ratio[:], scalar2=None, op0=ALU.mult)
+
+        log(0)
+        for i in range(2):
+            bank = transpose_pair([w_raw[:, 2 * i, :], w_raw[:, 2 * i + 1, :]])
+            unload(bank, w_grp, 256 * i)
+        log(1)
+        quantize(w_grp, w_code, w_exp, 0, K)
+        for i in range(4):
+            bank = transpose_pair([p_raw[:, 2 * i, :], p_raw[:, 2 * i + 1, :]])
+            unload(bank, p_grp, 256 * i)
+        exponent(0)
+        quantize(p_grp, p_code, p_exp, 0, 512)
+        log(2)
+        exponent(1)
+        quantize(p_grp, p_code, p_exp, 512, NODES)
+        for i in range(4):
+            bank = transpose_pair([q_val[:, 2 * i, :], q_val[:, 2 * i + 1, :]])
+            unload(bank, q_grp, 256 * i)
+            if i == 1:
+                log(3)
+        banks = [stage1(r) for r in range(4)]
+        add_bias(0, banks[0])
+        add_bias(1, banks[1])
+        exponent(2)
+        quantize(dec_grp, dec_code, dec_exp, 0, 256)
+        add_bias(2, banks[2])
+        add_bias(3, banks[3])
+        banks = [stage1(r) for r in range(4, 8)]
+        exponent(3)
+        quantize(dec_grp, dec_code, dec_exp, 256, 512)
+        add_bias(4, banks[0])
+        add_bias(5, banks[1])
+        quantize(q_grp, q_code, q_exp, 0, 512)
+        quantize(dec_grp, dec_code, dec_exp, 512, 768)
+        add_bias(6, banks[2])
+        add_bias(7, banks[3])
+        quantize(q_grp, q_code, q_exp, 512, NODES)
+        quantize(dec_grp, dec_code, dec_exp, 768, NODES)
+        for r in range(4, 8):
+            log(r)
+        e6 = exponent_pe(6)
+        for r in range(4, 6):
+            exponent(r)
+        for r in range(6):
+            exp(r)
+        exp_pe(6, e6)
+        for r in range(8):
+            banks = stage2(r)
+            if r == 1:
+                e7 = exponent_pe(7)
+                exp_pe(7, e7)
+            for h in range(2):
+                finish(r, h, banks[h])
+                if r == 7:
+                    qs = slice(h * 512, (h + 1) * 512)
+                    nc.sync.dma_start(out=o_dst[:, r, qs], in_=res[:, r, qs])
+            if r < 7:
+                nc.sync.dma_start(out=o_dst[:, r, :], in_=res[:, r, :])

@@ -67,23 +67,22 @@ def tile_gglr_pb_kernel(tc, p_last, q_bytes, q_scale, dist, wd, bd, a, b, c, out
         p_src = p_last.rearrange("(p r) k -> p r k", r=R)
         d_src = dist.rearrange("(p r) n -> p r n", r=R)
         o_dst = out.rearrange("(p r) n -> p r n", r=R)
-        nc.sync.dma_start(out=q_raw[:, 0:4, :], in_=q_src[:, 0:4, :])
         nc.sync.dma_start(out=d_raw[:, 0:1, :], in_=d_src[:, 0:1, :])
-        nc.sync.dma_start(out=w_raw[:], in_=wd.rearrange("(m t) k -> m t k", t=4))
-        nc.sync.dma_start(out=q_raw[:, 4:8, :], in_=q_src[:, 4:8, :])
+        nc.sync.dma_start(out=q_raw[:, 0:4, :], in_=q_src[:, 0:4, :])
         nc.sync.dma_start(out=d_raw[:, 1:2, :], in_=d_src[:, 1:2, :])
+        nc.sync.dma_start(out=w_raw[:], in_=wd.rearrange("(m t) k -> m t k", t=4))
         nc.sync.dma_start(out=p_raw[:, 0:4, :], in_=p_src[:, 0:4, :])
+        nc.sync.dma_start(out=q_raw[:, 4:8, :], in_=q_src[:, 4:8, :])
         nc.sync.dma_start(out=p_raw[:, 4:8, :], in_=p_src[:, 4:8, :])
         for r in range(2, R, 2):
             nc.sync.dma_start(out=d_raw[:, r : r + 2, :], in_=d_src[:, r : r + 2, :])
-        nc.scalar.dma_start(out=c_bf[:], in_=c.partition_broadcast(P))
-        nc.scalar.dma_start(out=b_bf[:], in_=b.partition_broadcast(P))
-        nc.scalar.dma_start(out=a_bf[:], in_=a.partition_broadcast(P))
-        nc.scalar.dma_start(out=bias[:], in_=bd.rearrange("(p t) -> p t", t=4))
-
         nc.vector.memset(warm[:], 1.0)
         nc.scalar.activation(out=warm[:], in_=warm[:], func=ACT.Ln)
         make_identity(nc, ident[:])
+        nc.gpsimd.dma_start(out=c_bf[:], in_=c.partition_broadcast(P))
+        nc.gpsimd.dma_start(out=b_bf[:], in_=b.partition_broadcast(P))
+        nc.gpsimd.dma_start(out=bias[:], in_=bd.rearrange("(p t) -> p t", t=4))
+        nc.gpsimd.dma_start(out=a_bf[:], in_=a.partition_broadcast(P))
         make_identity(nc, ident_bf[:])
 
         def transpose_pair(srcs):
@@ -116,6 +115,12 @@ def tile_gglr_pb_kernel(tc, p_last, q_bytes, q_scale, dist, wd, bd, a, b, c, out
             nc.vector.scalar_tensor_tensor(
                 out=lnd[:, r, :], in0=lnd[:, r, :], scalar=ratio[:], in1=d_raw[:, r, :], op0=ALU.mult, op1=ALU.add
             )
+
+        def exponent_gpsimd(r):
+            for h in range(2):
+                qs = slice(h * 512, (h + 1) * 512)
+                nc.gpsimd.tensor_scalar(out=lnd[:, r, qs], in0=lnd[:, r, qs], scalar1=ratio[:], scalar2=0.0, op0=ALU.mult, op1=ALU.add)
+                nc.gpsimd.tensor_tensor(out=lnd[:, r, qs], in0=lnd[:, r, qs], in1=d_raw[:, r, qs], op=ALU.add)
 
         def exponent_pe(r):
             banks = []
@@ -193,75 +198,89 @@ def tile_gglr_pb_kernel(tc, p_last, q_bytes, q_scale, dist, wd, bd, a, b, c, out
             out=scale_row[:].rearrange("p (j t) -> p j t", t=4), in_=bank[:].rearrange("p (t j) -> p j t", t=4)
         )
 
-        for r in range(4):
-            product(r)
+        product(0)
         nc.vector.tensor_scalar(out=c_abs[:], in0=c_bf[:], scalar1=-1.0, scalar2=None, op0=ALU.mult)
-        nc.vector.tensor_copy(out=gain[:], in_=a_bf[:])
+        product(1)
         nc.vector.tensor_tensor(out=c_abs[:], in0=c_abs[:], in1=c_bf[:], op=ALU.max)
-        product(4)
+        product(2)
         nc.vector.tensor_scalar(out=c_low[:], in0=c_abs[:], scalar1=1e-20, scalar2=2e-20, op0=ALU.is_lt, op1=ALU.mult)
-        product(5)
+        product(3)
         nc.vector.tensor_tensor(out=decay[:], in0=c_low[:], in1=c_bf[:], op=ALU.add)
-        product(6)
         nc.vector.reciprocal(out=c_inv[:], in_=decay[:])
-        product(7)
         nc.vector.tensor_tensor(out=ratio[:], in0=c_inv[:], in1=b_bf[:], op=ALU.mult)
-        nc.gpsimd.tensor_scalar(out=diag[:], in0=ident[:], scalar1=ratio[:], scalar2=None, op0=ALU.mult)
+        nc.gpsimd.tensor_scalar(out=diag[:], in0=ident[:], scalar1=ratio[:], scalar2=0.0, op0=ALU.mult, op1=ALU.add)
 
         log(0)
+        log(1)
         for i in range(2):
             bank = transpose_pair([w_raw[:, 2 * i, :], w_raw[:, 2 * i + 1, :]])
             unload(bank, w_grp, 256 * i)
-        log(1)
+        exponent(0)
         quantize(w_grp, w_code, w_exp, 0, K)
+        exponent_gpsimd(1)
+        product(4)
+        product(5)
         for i in range(4):
             bank = transpose_pair([p_raw[:, 2 * i, :], p_raw[:, 2 * i + 1, :]])
             unload(bank, p_grp, 256 * i)
-        exponent(0)
         quantize(p_grp, p_code, p_exp, 0, 512)
+        product(6)
         log(2)
-        exponent(1)
+        exponent_gpsimd(2)
         quantize(p_grp, p_code, p_exp, 512, NODES)
-        for i in range(4):
+        product(7)
+        nc.vector.tensor_copy(out=gain[:], in_=a_bf[:])
+        for i in range(2):
             bank = transpose_pair([q_val[:, 2 * i, :], q_val[:, 2 * i + 1, :]])
             unload(bank, q_grp, 256 * i)
-            if i == 1:
-                log(3)
+        log(3)
         banks = [stage1(r) for r in range(4)]
         add_bias(0, banks[0])
         add_bias(1, banks[1])
-        exponent(2)
-        quantize(dec_grp, dec_code, dec_exp, 0, 256)
         add_bias(2, banks[2])
+        quantize(dec_grp, dec_code, dec_exp, 0, 256)
         add_bias(3, banks[3])
+        log(4)
+        qbanks = [transpose_pair([q_val[:, 2 * i, :], q_val[:, 2 * i + 1, :]]) for i in (2, 3)]
         banks = [stage1(r) for r in range(4, 8)]
-        exponent(3)
-        quantize(dec_grp, dec_code, dec_exp, 256, 512)
+        e3 = exponent_pe(3)
+        e4 = exponent_pe(4)
         add_bias(4, banks[0])
+        quantize(dec_grp, dec_code, dec_exp, 256, 512)
         add_bias(5, banks[1])
         quantize(q_grp, q_code, q_exp, 0, 512)
         quantize(dec_grp, dec_code, dec_exp, 512, 768)
         add_bias(6, banks[2])
         add_bias(7, banks[3])
+        for i in range(2):
+            unload(qbanks[i], q_grp, 512 + 256 * i)
+        for r in range(5, 8):
+            log(r)
+        exponent(5)
         quantize(q_grp, q_code, q_exp, 512, NODES)
         quantize(dec_grp, dec_code, dec_exp, 768, NODES)
-        for r in range(4, 8):
-            log(r)
-        e6 = exponent_pe(6)
-        for r in range(4, 6):
-            exponent(r)
-        for r in range(6):
-            exp(r)
-        exp_pe(6, e6)
-        for r in range(8):
+        exponent(6)
+        exponent(7)
+        exp(0)
+        exp_pe(3, e3)
+        exp_pe(4, e4)
+        exp(1)
+        exp(5)
+        exp(2)
+        exp(6)
+        exp(7)
+        order = (0, 3, 4, 1, 5, 2, 6, 7)
+        for i, r in enumerate(order):
             banks = stage2(r)
-            if r == 1:
-                e7 = exponent_pe(7)
-                exp_pe(7, e7)
-            for h in range(2):
-                finish(r, h, banks[h])
-                if r == 7:
-                    qs = slice(h * 512, (h + 1) * 512)
-                    nc.sync.dma_start(out=o_dst[:, r, qs], in_=res[:, r, qs])
-            if r < 7:
+            finish(r, 0, banks[0])
+            if i < 7:
+                finish(r, 1, banks[1])
                 nc.sync.dma_start(out=o_dst[:, r, :], in_=res[:, r, :])
+            else:
+                nc.sync.dma_start(out=o_dst[:, r, :512], in_=res[:, r, :512])
+                for qs in (slice(0, 256), slice(256, 512)):
+                    ns = slice(512 + qs.start, 512 + qs.stop)
+                    nc.vector.scalar_tensor_tensor(
+                        out=res[:, r, ns], in0=banks[1][:, qs], scalar=gain[:], in1=fx[:, r, ns], op0=ALU.mult, op1=ALU.mult
+                    )
+                    nc.sync.dma_start(out=o_dst[:, r, ns], in_=res[:, r, ns])

@@ -67,22 +67,24 @@ def tile_gglr_pb_kernel(tc, p_last, q_bytes, q_scale, dist, wd, bd, a, b, c, out
         p_src = p_last.rearrange("(p r) k -> p r k", r=R)
         d_src = dist.rearrange("(p r) n -> p r n", r=R)
         o_dst = out.rearrange("(p r) n -> p r n", r=R)
+        nc.scalar.dma_start(out=c_bf[:], in_=c.partition_broadcast(P))
+        nc.scalar.dma_start(out=b_bf[:], in_=b.partition_broadcast(P))
         nc.sync.dma_start(out=d_raw[:, 0:1, :], in_=d_src[:, 0:1, :])
         nc.sync.dma_start(out=q_raw[:, 0:4, :], in_=q_src[:, 0:4, :])
         nc.sync.dma_start(out=d_raw[:, 1:2, :], in_=d_src[:, 1:2, :])
+        nc.sync.dma_start(out=d_raw[:, 2:3, :], in_=d_src[:, 2:3, :])
         nc.sync.dma_start(out=w_raw[:], in_=wd.rearrange("(m t) k -> m t k", t=4))
         nc.sync.dma_start(out=p_raw[:, 0:4, :], in_=p_src[:, 0:4, :])
         nc.sync.dma_start(out=q_raw[:, 4:8, :], in_=q_src[:, 4:8, :])
         nc.sync.dma_start(out=p_raw[:, 4:8, :], in_=p_src[:, 4:8, :])
-        for r in range(2, R, 2):
+        nc.sync.dma_start(out=d_raw[:, 3:4, :], in_=d_src[:, 3:4, :])
+        nc.sync.dma_start(out=bias[:], in_=bd.rearrange("(p t) -> p t", t=4))
+        nc.sync.dma_start(out=a_bf[:], in_=a.partition_broadcast(P))
+        for r in range(4, R, 2):
             nc.sync.dma_start(out=d_raw[:, r : r + 2, :], in_=d_src[:, r : r + 2, :])
         nc.vector.memset(warm[:], 1.0)
         nc.scalar.activation(out=warm[:], in_=warm[:], func=ACT.Ln)
         make_identity(nc, ident[:])
-        nc.gpsimd.dma_start(out=c_bf[:], in_=c.partition_broadcast(P))
-        nc.gpsimd.dma_start(out=b_bf[:], in_=b.partition_broadcast(P))
-        nc.gpsimd.dma_start(out=bias[:], in_=bd.rearrange("(p t) -> p t", t=4))
-        nc.gpsimd.dma_start(out=a_bf[:], in_=a.partition_broadcast(P))
         make_identity(nc, ident_bf[:])
 
         def transpose_pair(srcs):
@@ -122,20 +124,16 @@ def tile_gglr_pb_kernel(tc, p_last, q_bytes, q_scale, dist, wd, bd, a, b, c, out
                 nc.gpsimd.tensor_scalar(out=lnd[:, r, qs], in0=lnd[:, r, qs], scalar1=ratio[:], scalar2=0.0, op0=ALU.mult, op1=ALU.add)
                 nc.gpsimd.tensor_tensor(out=lnd[:, r, qs], in0=lnd[:, r, qs], in1=d_raw[:, r, qs], op=ALU.add)
 
-        def exponent_pe(r):
-            banks = []
-            for h in range(2):
-                bank = psum.tile([P, 512], F32, name="bank", tag="bank")
-                qs = slice(h * 512, (h + 1) * 512)
-                nc.tensor.matmul(bank[:], lhsT=ident_bf[:], rhs=d_raw[:, r, qs], start=True, stop=False)
-                nc.tensor.matmul(bank[:], lhsT=diag[:], rhs=lnd[:, r, qs], start=False, stop=True)
-                banks.append(bank)
-            return banks
+        def exponent_pe(r, h):
+            bank = psum.tile([P, 512], F32, name="bank", tag="bank")
+            qs = slice(h * 512, (h + 1) * 512)
+            nc.tensor.matmul(bank[:], lhsT=ident_bf[:], rhs=d_raw[:, r, qs], start=True, stop=False)
+            nc.tensor.matmul(bank[:], lhsT=diag[:], rhs=lnd[:, r, qs], start=False, stop=True)
+            return bank
 
-        def exp_pe(r, banks):
-            for h in range(2):
-                qs = slice(h * 512, (h + 1) * 512)
-                nc.scalar.activation(out=fx[:, r, qs], in_=banks[h][:], func=ACT.Exp, scale=decay[:])
+        def exp_pe(r, h, bank):
+            qs = slice(h * 512, (h + 1) * 512)
+            nc.scalar.activation(out=fx[:, r, qs], in_=bank[:], func=ACT.Exp, scale=decay[:])
 
         def exp(r):
             nc.scalar.activation(out=fx[:, r, :], in_=lnd[:, r, :], func=ACT.Exp, scale=decay[:])
@@ -212,27 +210,30 @@ def tile_gglr_pb_kernel(tc, p_last, q_bytes, q_scale, dist, wd, bd, a, b, c, out
 
         log(0)
         log(1)
-        for i in range(2):
-            bank = transpose_pair([w_raw[:, 2 * i, :], w_raw[:, 2 * i + 1, :]])
-            unload(bank, w_grp, 256 * i)
+        log(2)
+        w_banks = [transpose_pair([w_raw[:, 2 * i, :], w_raw[:, 2 * i + 1, :]]) for i in range(2)]
+        p_banks = [transpose_pair([p_raw[:, 2 * i, :], p_raw[:, 2 * i + 1, :]]) for i in range(2)]
+        q_banks = [transpose_pair([q_val[:, 2 * i, :], q_val[:, 2 * i + 1, :]]) for i in range(2)]
+        p_banks += [transpose_pair([p_raw[:, 2 * i, :], p_raw[:, 2 * i + 1, :]]) for i in range(2, 4)]
+        unload(w_banks[0], w_grp, 0)
+        unload(w_banks[1], w_grp, 256)
         exponent(0)
-        quantize(w_grp, w_code, w_exp, 0, K)
         exponent_gpsimd(1)
+        exponent_gpsimd(2)
+        quantize(w_grp, w_code, w_exp, 0, K)
+        unload(p_banks[0], p_grp, 0)
+        unload(p_banks[1], p_grp, 256)
         product(4)
         product(5)
-        for i in range(4):
-            bank = transpose_pair([p_raw[:, 2 * i, :], p_raw[:, 2 * i + 1, :]])
-            unload(bank, p_grp, 256 * i)
         quantize(p_grp, p_code, p_exp, 0, 512)
+        unload(q_banks[0], q_grp, 0)
+        unload(q_banks[1], q_grp, 256)
         product(6)
-        log(2)
-        exponent_gpsimd(2)
-        quantize(p_grp, p_code, p_exp, 512, NODES)
         product(7)
+        unload(p_banks[2], p_grp, 512)
+        unload(p_banks[3], p_grp, 768)
+        quantize(p_grp, p_code, p_exp, 512, NODES)
         nc.vector.tensor_copy(out=gain[:], in_=a_bf[:])
-        for i in range(2):
-            bank = transpose_pair([q_val[:, 2 * i, :], q_val[:, 2 * i + 1, :]])
-            unload(bank, q_grp, 256 * i)
         log(3)
         banks = [stage1(r) for r in range(4)]
         add_bias(0, banks[0])
@@ -241,10 +242,9 @@ def tile_gglr_pb_kernel(tc, p_last, q_bytes, q_scale, dist, wd, bd, a, b, c, out
         quantize(dec_grp, dec_code, dec_exp, 0, 256)
         add_bias(3, banks[3])
         log(4)
-        qbanks = [transpose_pair([q_val[:, 2 * i, :], q_val[:, 2 * i + 1, :]]) for i in (2, 3)]
+        q_banks = [transpose_pair([q_val[:, 2 * i, :], q_val[:, 2 * i + 1, :]]) for i in (2, 3)]
         banks = [stage1(r) for r in range(4, 8)]
-        e3 = exponent_pe(3)
-        e4 = exponent_pe(4)
+        e_banks = {(3, 0): exponent_pe(3, 0), (3, 1): exponent_pe(3, 1), (4, 0): exponent_pe(4, 0)}
         add_bias(4, banks[0])
         quantize(dec_grp, dec_code, dec_exp, 256, 512)
         add_bias(5, banks[1])
@@ -252,26 +252,30 @@ def tile_gglr_pb_kernel(tc, p_last, q_bytes, q_scale, dist, wd, bd, a, b, c, out
         quantize(dec_grp, dec_code, dec_exp, 512, 768)
         add_bias(6, banks[2])
         add_bias(7, banks[3])
-        for i in range(2):
-            unload(qbanks[i], q_grp, 512 + 256 * i)
+        unload(q_banks[0], q_grp, 512)
+        unload(q_banks[1], q_grp, 768)
         for r in range(5, 8):
             log(r)
-        exponent(5)
+        exponent_gpsimd(5)
         quantize(q_grp, q_code, q_exp, 512, NODES)
         quantize(dec_grp, dec_code, dec_exp, 768, NODES)
         exponent(6)
         exponent(7)
         exp(0)
-        exp_pe(3, e3)
-        exp_pe(4, e4)
+        s2 = {0: stage2(0)}
+        e_banks[4, 1] = exponent_pe(4, 1)
+        exp_pe(3, 0, e_banks[3, 0])
+        exp_pe(3, 1, e_banks[3, 1])
+        exp_pe(4, 0, e_banks[4, 0])
+        exp_pe(4, 1, e_banks[4, 1])
         exp(1)
-        exp(5)
-        exp(2)
         exp(6)
+        exp(2)
         exp(7)
-        order = (0, 3, 4, 1, 5, 2, 6, 7)
+        exp(5)
+        order = (0, 3, 4, 1, 6, 2, 7, 5)
         for i, r in enumerate(order):
-            banks = stage2(r)
+            banks = s2[r] if r in s2 else stage2(r)
             finish(r, 0, banks[0])
             if i < 7:
                 finish(r, 1, banks[1])

@@ -63,19 +63,19 @@ def tile_gglr_pb_kernel(tc, p_last, q_bytes, q_scale, dist, wd, bd, a, b, c, out
         res = keep.tile([P, R, NODES], F32, align_bytes=64)
 
         nc.sync.dma_start(out=s4[:], in_=q_scale.rearrange("o (p t) -> p (o t)", t=4))
-        q_src = q_bytes.rearrange("(r p) k -> p r k", p=P)
+        q_src = q_bytes.rearrange("(h p e) k -> h p e k", h=2, e=4)
         p_src = p_last.rearrange("(p r) k -> p r k", r=R)
         d_src = dist.rearrange("(p r) n -> p r n", r=R)
         o_dst = out.rearrange("(p r) n -> p r n", r=R)
         nc.scalar.dma_start(out=c_bf[:], in_=c.partition_broadcast(P))
         nc.scalar.dma_start(out=b_bf[:], in_=b.partition_broadcast(P))
         nc.sync.dma_start(out=d_raw[:, 0:1, :], in_=d_src[:, 0:1, :])
-        nc.sync.dma_start(out=q_raw[:, 0:4, :], in_=q_src[:, 0:4, :])
+        nc.sync.dma_start(out=q_raw[:, 0:4, :], in_=q_src[0])
         nc.sync.dma_start(out=d_raw[:, 1:2, :], in_=d_src[:, 1:2, :])
         nc.sync.dma_start(out=d_raw[:, 2:3, :], in_=d_src[:, 2:3, :])
         nc.sync.dma_start(out=w_raw[:], in_=wd.rearrange("(m t) k -> m t k", t=4))
         nc.sync.dma_start(out=p_raw[:, 0:4, :], in_=p_src[:, 0:4, :])
-        nc.sync.dma_start(out=q_raw[:, 4:8, :], in_=q_src[:, 4:8, :])
+        nc.sync.dma_start(out=q_raw[:, 4:8, :], in_=q_src[1])
         nc.sync.dma_start(out=p_raw[:, 4:8, :], in_=p_src[:, 4:8, :])
         nc.sync.dma_start(out=d_raw[:, 3:4, :], in_=d_src[:, 3:4, :])
         nc.sync.dma_start(out=bias[:], in_=bd.rearrange("(p t) -> p t", t=4))
@@ -103,6 +103,13 @@ def tile_gglr_pb_kernel(tc, p_last, q_bytes, q_scale, dist, wd, bd, a, b, c, out
                 in_=bank[:].rearrange("p (u j) -> p j u", u=2),
             )
 
+        def unload_q(bank, half, i):
+            dst = q_grp[:, half * 512 : (half + 1) * 512, :].rearrange("p j e -> p (j e)").bitcast(F32)
+            nc.scalar.copy(
+                out=dst.rearrange("p (j e u) -> p j e u", e=4, u=2)[:, :, 2 * i : 2 * i + 2, :],
+                in_=bank[:].rearrange("p (u e j) -> p j e u", u=2, e=2),
+            )
+
         def quantize(grp, code, exps, lo, hi):
             nc.vector.quantize_mx(
                 out=code[:, lo:hi].bitcast(FP8X4),
@@ -119,17 +126,22 @@ def tile_gglr_pb_kernel(tc, p_last, q_bytes, q_scale, dist, wd, bd, a, b, c, out
             )
 
         def exponent_gpsimd(r):
-            for h in range(2):
-                qs = slice(h * 512, (h + 1) * 512)
+            for lo in (0, 512):
+                qs = slice(lo, lo + 512)
                 nc.gpsimd.tensor_scalar(out=lnd[:, r, qs], in0=lnd[:, r, qs], scalar1=ratio[:], scalar2=0.0, op0=ALU.mult, op1=ALU.add)
+            for lo in range(0, NODES, 256):
+                qs = slice(lo, lo + 256)
                 nc.gpsimd.tensor_tensor(out=lnd[:, r, qs], in0=lnd[:, r, qs], in1=d_raw[:, r, qs], op=ALU.add)
 
-        def exponent_pe(r, h):
+        def open_exponent(r, h):
             bank = psum.tile([P, 512], F32, name="bank", tag="bank")
             qs = slice(h * 512, (h + 1) * 512)
             nc.tensor.matmul(bank[:], lhsT=ident_bf[:], rhs=d_raw[:, r, qs], start=True, stop=False)
-            nc.tensor.matmul(bank[:], lhsT=diag[:], rhs=lnd[:, r, qs], start=False, stop=True)
             return bank
+
+        def close_exponent(r, h, bank):
+            qs = slice(h * 512, (h + 1) * 512)
+            nc.tensor.matmul(bank[:], lhsT=diag[:], rhs=lnd[:, r, qs], start=False, stop=True)
 
         def exp_pe(r, h, bank):
             qs = slice(h * 512, (h + 1) * 512)
@@ -196,45 +208,48 @@ def tile_gglr_pb_kernel(tc, p_last, q_bytes, q_scale, dist, wd, bd, a, b, c, out
             out=scale_row[:].rearrange("p (j t) -> p j t", t=4), in_=bank[:].rearrange("p (t j) -> p j t", t=4)
         )
 
-        product(0)
         nc.vector.tensor_scalar(out=c_abs[:], in0=c_bf[:], scalar1=-1.0, scalar2=None, op0=ALU.mult)
-        product(1)
         nc.vector.tensor_tensor(out=c_abs[:], in0=c_abs[:], in1=c_bf[:], op=ALU.max)
-        product(2)
+        product(0)
         nc.vector.tensor_scalar(out=c_low[:], in0=c_abs[:], scalar1=1e-20, scalar2=2e-20, op0=ALU.is_lt, op1=ALU.mult)
-        product(3)
+        product(1)
         nc.vector.tensor_tensor(out=decay[:], in0=c_low[:], in1=c_bf[:], op=ALU.add)
+        product(2)
         nc.vector.reciprocal(out=c_inv[:], in_=decay[:])
+        product(3)
         nc.vector.tensor_tensor(out=ratio[:], in0=c_inv[:], in1=b_bf[:], op=ALU.mult)
         nc.gpsimd.tensor_scalar(out=diag[:], in0=ident[:], scalar1=ratio[:], scalar2=0.0, op0=ALU.mult, op1=ALU.add)
+
+        def turn(raw, i):
+            return transpose_pair([raw[:, 2 * i, :], raw[:, 2 * i + 1, :]])
 
         log(0)
         log(1)
         log(2)
-        w_banks = [transpose_pair([w_raw[:, 2 * i, :], w_raw[:, 2 * i + 1, :]]) for i in range(2)]
-        p_banks = [transpose_pair([p_raw[:, 2 * i, :], p_raw[:, 2 * i + 1, :]]) for i in range(2)]
-        q_banks = [transpose_pair([q_val[:, 2 * i, :], q_val[:, 2 * i + 1, :]]) for i in range(2)]
-        p_banks += [transpose_pair([p_raw[:, 2 * i, :], p_raw[:, 2 * i + 1, :]]) for i in range(2, 4)]
+        w_banks = [turn(w_raw, i) for i in range(2)]
+        p_banks = [turn(p_raw, i) for i in range(2)]
+        q_banks = [turn(q_val, i) for i in range(2)]
+        p_banks += [turn(p_raw, i) for i in range(2, 4)]
+        exponent(0)
         unload(w_banks[0], w_grp, 0)
         unload(w_banks[1], w_grp, 256)
-        exponent(0)
-        exponent_gpsimd(1)
-        exponent_gpsimd(2)
+        exponent(1)
         quantize(w_grp, w_code, w_exp, 0, K)
         unload(p_banks[0], p_grp, 0)
         unload(p_banks[1], p_grp, 256)
         product(4)
         product(5)
         quantize(p_grp, p_code, p_exp, 0, 512)
-        unload(q_banks[0], q_grp, 0)
-        unload(q_banks[1], q_grp, 256)
-        product(6)
-        product(7)
+        unload_q(q_banks[0], 0, 0)
+        unload_q(q_banks[1], 0, 1)
         unload(p_banks[2], p_grp, 512)
         unload(p_banks[3], p_grp, 768)
+        product(6)
+        product(7)
         quantize(p_grp, p_code, p_exp, 512, NODES)
         nc.vector.tensor_copy(out=gain[:], in_=a_bf[:])
         log(3)
+        exponent_gpsimd(3)
         banks = [stage1(r) for r in range(4)]
         add_bias(0, banks[0])
         add_bias(1, banks[1])
@@ -242,9 +257,12 @@ def tile_gglr_pb_kernel(tc, p_last, q_bytes, q_scale, dist, wd, bd, a, b, c, out
         quantize(dec_grp, dec_code, dec_exp, 0, 256)
         add_bias(3, banks[3])
         log(4)
-        q_banks = [transpose_pair([q_val[:, 2 * i, :], q_val[:, 2 * i + 1, :]]) for i in (2, 3)]
+        q_banks = [turn(q_val, i) for i in (2, 3)]
         banks = [stage1(r) for r in range(4, 8)]
-        e_banks = {(3, 0): exponent_pe(3, 0), (3, 1): exponent_pe(3, 1), (4, 0): exponent_pe(4, 0)}
+        e_banks = {(r, h): open_exponent(r, h) for r in (2, 4) for h in range(2)}
+        close_exponent(2, 0, e_banks[2, 0])
+        close_exponent(2, 1, e_banks[2, 1])
+        close_exponent(4, 0, e_banks[4, 0])
         add_bias(4, banks[0])
         quantize(dec_grp, dec_code, dec_exp, 256, 512)
         add_bias(5, banks[1])
@@ -252,32 +270,37 @@ def tile_gglr_pb_kernel(tc, p_last, q_bytes, q_scale, dist, wd, bd, a, b, c, out
         quantize(dec_grp, dec_code, dec_exp, 512, 768)
         add_bias(6, banks[2])
         add_bias(7, banks[3])
-        unload(q_banks[0], q_grp, 512)
-        unload(q_banks[1], q_grp, 768)
-        for r in range(5, 8):
-            log(r)
+        log(5)
         exponent_gpsimd(5)
+        unload_q(q_banks[0], 1, 0)
+        unload_q(q_banks[1], 1, 1)
+        log(6)
+        exponent_gpsimd(6)
+        log(7)
         quantize(q_grp, q_code, q_exp, 512, NODES)
         quantize(dec_grp, dec_code, dec_exp, 768, NODES)
-        exponent(6)
         exponent(7)
         exp(0)
-        s2 = {0: stage2(0)}
-        e_banks[4, 1] = exponent_pe(4, 1)
-        exp_pe(3, 0, e_banks[3, 0])
-        exp_pe(3, 1, e_banks[3, 1])
+        s2 = {0: stage2(0), 2: stage2(2)}
+        close_exponent(4, 1, e_banks[4, 1])
+        exp_pe(2, 0, e_banks[2, 0])
+        exp_pe(2, 1, e_banks[2, 1])
+        exp(1)
         exp_pe(4, 0, e_banks[4, 0])
         exp_pe(4, 1, e_banks[4, 1])
-        exp(1)
-        exp(6)
-        exp(2)
+        exp(3)
         exp(7)
         exp(5)
-        order = (0, 3, 4, 1, 6, 2, 7, 5)
+        exp(6)
+        order = (0, 2, 1, 4, 3, 7, 5, 6)
         for i, r in enumerate(order):
             banks = s2[r] if r in s2 else stage2(r)
             finish(r, 0, banks[0])
-            if i < 7:
+            if i == 0:
+                nc.sync.dma_start(out=o_dst[:, r, :512], in_=res[:, r, :512])
+                finish(r, 1, banks[1])
+                nc.sync.dma_start(out=o_dst[:, r, 512:], in_=res[:, r, 512:])
+            elif i < 7:
                 finish(r, 1, banks[1])
                 nc.sync.dma_start(out=o_dst[:, r, :], in_=res[:, r, :])
             else:

from contextlib import ExitStack

import concourse.mybir as mybir
from concourse.masks import make_identity

NODES, K = 1024, 512
P = 128
R = NODES // P
FLOPS = 2 * NODES * K * K + 2 * NODES * NODES * K

F32 = mybir.dt.float32
BF16 = mybir.dt.bfloat16
U32 = mybir.dt.uint32
U8 = mybir.dt.uint8
FP8 = mybir.dt.float8_e4m3fn
FP8X4 = mybir.dt.float8_e4m3fn_x4
ALU = mybir.AluOpType
ACT = mybir.ActivationFunctionType


def tile_gglr_pb_kernel(tc, p_last, q_bytes, q_scale, dist, wd, bd, a, b, c, out):
    nc = tc.nc
    with ExitStack() as ctx:
        keep = ctx.enter_context(tc.tile_pool(name="keep", bufs=1))
        psum = ctx.enter_context(tc.psum_pool(name="psum", bufs=8))
        ctx.enter_context(tc.manual_schedule())

        ident = keep.tile([P, P], F32)
        ident_bf = keep.tile([P, P], BF16)
        diag = keep.tile([P, P], F32)
        warm = keep.tile([P, 1], F32)
        s4 = keep.tile([P, 4], F32)
        bias = keep.tile([P, 4], BF16)
        a_bf = keep.tile([P, 1], BF16)
        b_bf = keep.tile([P, 1], BF16)
        c_bf = keep.tile([P, 1], BF16)
        gain = keep.tile([P, 1], F32)
        c_abs = keep.tile([P, 1], F32)
        c_low = keep.tile([P, 1], F32)
        decay = keep.tile([P, 1], F32)
        c_inv = keep.tile([P, 1], F32)
        ratio = keep.tile([P, 1], F32)
        scale_row = keep.tile([P, K], F32, align_bytes=64)
        q_raw = keep.tile([P, R, K], U8, align_bytes=64)
        q_val = keep.tile([P, R, K], BF16, align_bytes=64)
        w_raw = keep.tile([P, 4, K], BF16, align_bytes=64)
        p_raw = keep.tile([P, R, K], BF16, align_bytes=64)
        d_raw = keep.tile([P, R, NODES], BF16, align_bytes=64)
        w_grp = keep.tile([P, K, 4], BF16, align_bytes=64)
        p_grp = keep.tile([P, NODES, 4], BF16, align_bytes=64)
        q_grp = keep.tile([P, NODES, 4], BF16, align_bytes=64)
        dec_grp = keep.tile([P, NODES, 4], BF16, align_bytes=64)
        w_code = keep.tile([P, K], U32, align_bytes=64)
        w_exp = keep.tile([P, K], U8, align_bytes=64)
        p_code = keep.tile([P, NODES], U32, align_bytes=64)
        p_exp = keep.tile([P, NODES], U8, align_bytes=64)
        q_code = keep.tile([P, NODES], U32, align_bytes=64)
        q_exp = keep.tile([P, NODES], U8, align_bytes=64)
        dec_code = keep.tile([P, NODES], U32, align_bytes=64)
        dec_exp = keep.tile([P, NODES], U8, align_bytes=64)
        lnd = keep.tile([P, R, NODES], F32, align_bytes=64)
        fx = keep.tile([P, R, NODES], F32, align_bytes=64)
        res = keep.tile([P, R, NODES], F32, align_bytes=64)

        nc.sync.dma_start(out=s4[:], in_=q_scale.rearrange("o (p t) -> p (o t)", t=4))
        q_src = q_bytes.rearrange("(h p e) k -> h p e k", h=2, e=4)
        p_src = p_last.rearrange("(p r) k -> p r k", r=R)
        d_src = dist.rearrange("(p r) n -> p r n", r=R)
        o_dst = out.rearrange("(p r) n -> p r n", r=R)
        nc.scalar.dma_start(out=c_bf[:], in_=c.partition_broadcast(P))
        nc.scalar.dma_start(out=b_bf[:], in_=b.partition_broadcast(P))
        nc.sync.dma_start(out=d_raw[:, 0:1, :], in_=d_src[:, 0:1, :])
        nc.sync.dma_start(out=q_raw[:, 0:4, :], in_=q_src[0])
        nc.sync.dma_start(out=d_raw[:, 1:2, :], in_=d_src[:, 1:2, :])
        nc.sync.dma_start(out=d_raw[:, 2:3, :], in_=d_src[:, 2:3, :])
        nc.sync.dma_start(out=w_raw[:], in_=wd.rearrange("(m t) k -> m t k", t=4))
        nc.sync.dma_start(out=p_raw[:, 0:4, :], in_=p_src[:, 0:4, :])
        nc.sync.dma_start(out=q_raw[:, 4:8, :], in_=q_src[1])
        nc.sync.dma_start(out=p_raw[:, 4:8, :], in_=p_src[:, 4:8, :])
        nc.sync.dma_start(out=d_raw[:, 3:4, :], in_=d_src[:, 3:4, :])
        nc.sync.dma_start(out=bias[:], in_=bd.rearrange("(p t) -> p t", t=4))
        nc.sync.dma_start(out=a_bf[:], in_=a.partition_broadcast(P))
        for r in range(4, R, 2):
            nc.sync.dma_start(out=d_raw[:, r : r + 2, :], in_=d_src[:, r : r + 2, :])
        nc.vector.memset(warm[:], 1.0)
        nc.scalar.activation(out=warm[:], in_=warm[:], func=ACT.Ln)
        make_identity(nc, ident[:])
        make_identity(nc, ident_bf[:])

        def transpose_pair(srcs):
            bank = psum.tile([P, 512], F32, name="bank", tag="bank")
            halves = bank[:].rearrange("p (u j) -> p u j", u=2)
            for i, src in enumerate(srcs):
                words = src.bitcast(F32)
                for u in range(2):
                    nc.tensor.transpose(halves[:, u, i * P : (i + 1) * P], words[:, u::2], ident[:])
            return bank

        def unload(bank, grp, col):
            dst = grp[:, col : col + 256, :].rearrange("p j e -> p (j e)").bitcast(F32)
            nc.scalar.copy(
                out=dst.rearrange("p (j u) -> p j u", u=2),
                in_=bank[:].rearrange("p (u j) -> p j u", u=2),
            )

        def unload_q(bank, half, i):
            dst = q_grp[:, half * 512 : (half + 1) * 512, :].rearrange("p j e -> p (j e)").bitcast(F32)
            nc.scalar.copy(
                out=dst.rearrange("p (j e u) -> p j e u", e=4, u=2)[:, :, 2 * i : 2 * i + 2, :],
                in_=bank[:].rearrange("p (u e j) -> p j e u", u=2, e=2),
            )

        def quantize(grp, code, exps, lo, hi):
            nc.vector.quantize_mx(
                out=code[:, lo:hi].bitcast(FP8X4),
                scales=exps[:, lo:hi],
                in_=grp[:, lo:hi, :].rearrange("p j e -> p (j e)"),
            )

        def log(r):
            nc.scalar.activation(out=lnd[:, r, :], in_=d_raw[:, r, :], func=ACT.Ln)

        def exponent(r):
            nc.vector.scalar_tensor_tensor(
                out=lnd[:, r, :], in0=lnd[:, r, :], scalar=ratio[:], in1=d_raw[:, r, :], op0=ALU.mult, op1=ALU.add
            )

        def exponent_gpsimd(r):
            for lo in (0, 512):
                qs = slice(lo, lo + 512)
                nc.gpsimd.tensor_scalar(out=lnd[:, r, qs], in0=lnd[:, r, qs], scalar1=ratio[:], scalar2=0.0, op0=ALU.mult, op1=ALU.add)
            for lo in range(0, NODES, 256):
                qs = slice(lo, lo + 256)
                nc.gpsimd.tensor_tensor(out=lnd[:, r, qs], in0=lnd[:, r, qs], in1=d_raw[:, r, qs], op=ALU.add)

        def open_exponent(r, h):
            bank = psum.tile([P, 512], F32, name="bank", tag="bank")
            qs = slice(h * 512, (h + 1) * 512)
            nc.tensor.matmul(bank[:], lhsT=ident_bf[:], rhs=d_raw[:, r, qs], start=True, stop=False)
            return bank

        def close_exponent(r, h, bank):
            qs = slice(h * 512, (h + 1) * 512)
            nc.tensor.matmul(bank[:], lhsT=diag[:], rhs=lnd[:, r, qs], start=False, stop=True)

        def exp_pe(r, h, bank):
            qs = slice(h * 512, (h + 1) * 512)
            nc.scalar.activation(out=fx[:, r, qs], in_=bank[:], func=ACT.Exp, scale=decay[:])

        def exp(r):
            nc.scalar.activation(out=fx[:, r, :], in_=lnd[:, r, :], func=ACT.Exp, scale=decay[:])

        def product(r):
            nc.vector.tensor_tensor(out=q_val[:, r, :], in0=q_raw[:, r, :].bitcast(FP8), in1=scale_row[:], op=ALU.mult)

        def stage1(r):
            bank = psum.tile([P, 512], F32, name="bank", tag="bank")
            cols = slice(r * P, (r + 1) * P)
            for t in range(4):
                ws = slice(t * P, (t + 1) * P)
                nc.tensor.matmul_mx(
                    out=bank[:, ws],
                    lhsT=w_code[:, ws].bitcast(FP8X4),
                    lhsT_scale=w_exp[:, ws],
                    rhs=p_code[:, cols].bitcast(FP8X4),
                    rhs_scale=p_exp[:, cols],
                    start=True,
                    stop=True,
                )
            return bank

        def add_bias(r, bank):
            nc.vector.tensor_tensor(
                out=dec_grp[:, r * P : (r + 1) * P, :],
                in0=bank[:].rearrange("p (t j) -> p j t", t=4),
                in1=bias[:].unsqueeze(1).to_broadcast([P, P, 4]),
                op=ALU.add,
            )

        def stage2(r):
            cols = slice(r * P, (r + 1) * P)
            banks = []
            for h in range(2):
                bank = psum.tile([P, 512], F32, name="bank", tag="bank")
                qs = slice(h * 512, (h + 1) * 512)
                nc.tensor.matmul_mx(
                    out=bank[:],
                    lhsT=dec_code[:, cols].bitcast(FP8X4),
                    lhsT_scale=dec_exp[:, cols],
                    rhs=q_code[:, qs].bitcast(FP8X4),
                    rhs_scale=q_exp[:, qs],
                    start=True,
                    stop=True,
                )
                banks.append(bank)
            return banks

        def finish(r, h, bank):
            qs = slice(h * 512, (h + 1) * 512)
            nc.vector.scalar_tensor_tensor(
                out=res[:, r, qs], in0=bank[:], scalar=gain[:], in1=fx[:, r, qs], op0=ALU.mult, op1=ALU.mult
            )

        bank = psum.tile([P, 512], F32, name="bank", tag="bank")
        for t in range(4):
            nc.tensor.transpose(bank[:, t * P : (t + 1) * P], s4[:, t : t + 1].to_broadcast([P, P]), ident[:])
        nc.vector.tensor_copy(
            out=scale_row[:].rearrange("p (j t) -> p j t", t=4), in_=bank[:].rearrange("p (t j) -> p j t", t=4)
        )

        nc.vector.tensor_scalar(out=c_abs[:], in0=c_bf[:], scalar1=-1.0, scalar2=None, op0=ALU.mult)
        nc.vector.tensor_tensor(out=c_abs[:], in0=c_abs[:], in1=c_bf[:], op=ALU.max)
        product(0)
        nc.vector.tensor_scalar(out=c_low[:], in0=c_abs[:], scalar1=1e-20, scalar2=2e-20, op0=ALU.is_lt, op1=ALU.mult)
        product(1)
        nc.vector.tensor_tensor(out=decay[:], in0=c_low[:], in1=c_bf[:], op=ALU.add)
        product(2)
        nc.vector.reciprocal(out=c_inv[:], in_=decay[:])
        product(3)
        nc.vector.tensor_tensor(out=ratio[:], in0=c_inv[:], in1=b_bf[:], op=ALU.mult)
        nc.gpsimd.tensor_scalar(out=diag[:], in0=ident[:], scalar1=ratio[:], scalar2=0.0, op0=ALU.mult, op1=ALU.add)

        def turn(raw, i):
            return transpose_pair([raw[:, 2 * i, :], raw[:, 2 * i + 1, :]])

        log(0)
        log(1)
        log(2)
        w_banks = [turn(w_raw, i) for i in range(2)]
        p_banks = [turn(p_raw, i) for i in range(2)]
        q_banks = [turn(q_val, i) for i in range(2)]
        p_banks += [turn(p_raw, i) for i in range(2, 4)]
        exponent(0)
        unload(w_banks[0], w_grp, 0)
        unload(w_banks[1], w_grp, 256)
        exponent(1)
        quantize(w_grp, w_code, w_exp, 0, K)
        unload(p_banks[0], p_grp, 0)
        unload(p_banks[1], p_grp, 256)
        product(4)
        product(5)
        quantize(p_grp, p_code, p_exp, 0, 512)
        unload_q(q_banks[0], 0, 0)
        unload_q(q_banks[1], 0, 1)
        unload(p_banks[2], p_grp, 512)
        unload(p_banks[3], p_grp, 768)
        product(6)
        product(7)
        quantize(p_grp, p_code, p_exp, 512, NODES)
        nc.vector.tensor_copy(out=gain[:], in_=a_bf[:])
        log(3)
        exponent_gpsimd(3)
        banks = [stage1(r) for r in range(4)]
        add_bias(0, banks[0])
        add_bias(1, banks[1])
        add_bias(2, banks[2])
        quantize(dec_grp, dec_code, dec_exp, 0, 256)
        add_bias(3, banks[3])
        log(4)
        q_banks = [turn(q_val, i) for i in (2, 3)]
        banks = [stage1(r) for r in range(4, 8)]
        e_banks = {(r, h): open_exponent(r, h) for r in (2, 4) for h in range(2)}
        close_exponent(2, 0, e_banks[2, 0])
        close_exponent(2, 1, e_banks[2, 1])
        close_exponent(4, 0, e_banks[4, 0])
        add_bias(4, banks[0])
        quantize(dec_grp, dec_code, dec_exp, 256, 512)
        add_bias(5, banks[1])
        quantize(q_grp, q_code, q_exp, 0, 512)
        quantize(dec_grp, dec_code, dec_exp, 512, 768)
        add_bias(6, banks[2])
        add_bias(7, banks[3])
        log(5)
        exponent_gpsimd(5)
        unload_q(q_banks[0], 1, 0)
        unload_q(q_banks[1], 1, 1)
        log(6)
        exponent_gpsimd(6)
        log(7)
        quantize(q_grp, q_code, q_exp, 512, NODES)
        quantize(dec_grp, dec_code, dec_exp, 768, NODES)
        exponent(7)
        exp(0)
        s2 = {0: stage2(0), 2: stage2(2)}
        close_exponent(4, 1, e_banks[4, 1])
        exp_pe(2, 0, e_banks[2, 0])
        exp_pe(2, 1, e_banks[2, 1])
        exp(1)
        exp_pe(4, 0, e_banks[4, 0])
        exp_pe(4, 1, e_banks[4, 1])
        exp(3)
        exp(7)
        exp(5)
        exp(6)
        order = (0, 2, 1, 4, 3, 7, 5, 6)
        for i, r in enumerate(order):
            banks = s2[r] if r in s2 else stage2(r)
            finish(r, 0, banks[0])
            if i == 0:
                nc.sync.dma_start(out=o_dst[:, r, :512], in_=res[:, r, :512])
                finish(r, 1, banks[1])
                nc.sync.dma_start(out=o_dst[:, r, 512:], in_=res[:, r, 512:])
            elif i < 7:
                finish(r, 1, banks[1])
                nc.sync.dma_start(out=o_dst[:, r, :], in_=res[:, r, :])
            else:
                nc.sync.dma_start(out=o_dst[:, r, :512], in_=res[:, r, :512])
                for qs in (slice(0, 256), slice(256, 512)):
                    ns = slice(512 + qs.start, 512 + qs.stop)
                    nc.vector.scalar_tensor_tensor(
                        out=res[:, r, ns], in0=banks[1][:, qs], scalar=gain[:], in1=fx[:, r, ns], op0=ALU.mult, op1=ALU.mult
                    )
                    nc.sync.dma_start(out=o_dst[:, r, ns], in_=res[:, r, ns])
